import numpy as np
import ml_dtypes


def mxq(x, axis, fmt="e4m3"):
    dtype, down = {"e4m3": (ml_dtypes.float8_e4m3fn, 7), "e5m2": (ml_dtypes.float8_e5m2, 14)}[fmt]
    v = np.moveaxis(np.asarray(x, np.float32).astype(ml_dtypes.bfloat16).astype(np.float64), axis, -1)
    blocks = v.reshape(v.shape[:-1] + (-1, 32))
    amax = np.abs(blocks).max(-1, keepdims=True)
    byte = np.maximum(np.where(amax > 0, np.frexp(amax)[1] - 1 + 127, 0) - down, 1)
    scale = np.exp2(byte - 127.0)
    codes = (blocks / scale).astype(np.float32).astype(dtype).astype(np.float64)
    return np.moveaxis((codes * scale).reshape(v.shape), -1, axis)


WIDE = False


def mx_kscale(k):
    if not WIDE:
        return np.ones(k)
    levels = np.array([30, -30])
    if k % 512:
        return np.exp2(np.random.permutation(np.resize(levels, k // 32))).repeat(32)
    a = np.empty((k // 512, 16))
    for p in range(k // 512):
        a[p, :8] = np.random.permutation(np.resize(levels, 8))
        for g in range(8):
            far = levels[np.abs(levels - a[p, g]) >= 10]
            a[p, g + 8] = far[np.random.randint(len(far))]
    return np.exp2(a.ravel()).repeat(32)


BF16 = ml_dtypes.bfloat16


def bf(x):
    return np.asarray(x, np.float32).astype(BF16)


def f64(x):
    return np.asarray(x).astype(np.float64)


E2M1 = np.array([0.0, 0.5, 1.0, 1.5, 2.0, 3.0, 4.0, 6.0, -0.0, -0.5, -1.0, -1.5, -2.0, -3.0, -4.0, -6.0])


def pack_weight(w, fmt):
    k, n = w.shape
    w = f64(bf(w)).reshape(k // 32, 32, n)
    amax = np.abs(w).max(1)
    if fmt == "e4m3":
        byte = np.frexp(amax)[1] - 1 + 127 - 7
    else:
        mant, ex = np.frexp(amax / 6.0)
        byte = np.where(mant > 0.5, ex, ex - 1) + 127
    byte = np.clip(np.where(amax > 0, byte, 1), 1, 254)
    scaled = (w * np.exp2(127.0 - byte)[:, None, :]).reshape(k, n).astype(np.float32)
    by_word = np.ascontiguousarray(scaled.reshape(k // 512, 128, 4, n).transpose(0, 1, 3, 2))
    if fmt == "e4m3":
        words = by_word.astype(ml_dtypes.float8_e4m3fn).view(np.uint8)
    else:
        c = by_word.astype(ml_dtypes.float4_e2m1fn).view(np.uint8) & 0xF
        words = c[..., 0::2] | (c[..., 1::2] << 4)
    return np.ascontiguousarray(words), np.ascontiguousarray(byte.astype(np.uint8).reshape(k // 512, 16, n))


def unpack_weight(words, scales, fmt):
    g, p, n, _ = words.shape
    if fmt == "e4m3":
        vals = np.ascontiguousarray(words).view(ml_dtypes.float8_e4m3fn).astype(np.float64)
    else:
        nib = np.empty((g, p, n, 4), np.uint8)
        nib[..., 0::2] = words & 0xF
        nib[..., 1::2] = words >> 4
        vals = E2M1[nib]
    vals = vals * np.repeat(np.exp2(scales.astype(np.float64) - 127.0), 8, axis=1)[..., None]
    return vals.transpose(0, 1, 3, 2).reshape(g * 512, n)

def pack4(w):
    words, scales = pack_weight(w, "e2m1")
    return words.reshape(words.shape[0], 128, -1), scales


def unpack4(words, scales):
    return unpack_weight(words.reshape(words.shape[0], 128, -1, 2), scales, "e2m1")


B, T, D, H, KV, DH = 2, 256, 2048, 16, 4, 128
THETA = 1000000.0
EPS = 1e-6
HALF = DH // 2


def rms_norm(u, w):
    return w * u / np.sqrt(np.mean(u * u, axis=-1, keepdims=True) + EPS)


def rope(u):
    timescale = THETA ** (2.0 * np.arange(HALF) / DH)
    ang = (np.arange(T)[:, None] / timescale[None, :])[None, :, None, :]
    sin, cos = np.sin(ang), np.cos(ang)
    a, b = u[..., :HALF], u[..., HALF:]
    return np.concatenate([a * cos - b * sin, b * cos + a * sin], axis=-1)


def setup_inputs():
    s = mx_kscale(D)
    small = 3.0 * np.sqrt(EPS / D)
    x = bf(np.random.standard_normal((B, T, D)) * s)
    wq_words, wq_scales = pack4(np.random.standard_normal((D, H * DH)) * small / s[:, None])
    wk_words, wk_scales = pack4(np.random.standard_normal((D, KV * DH)) * small / s[:, None])
    wv_words, wv_scales = pack4(np.random.standard_normal((D, KV * DH)) / np.sqrt(D) / s[:, None])
    q_norm_w = bf(1.0 + 0.1 * np.random.standard_normal(DH))
    k_norm_w = bf(1.0 + 0.1 * np.random.standard_normal(DH))
    return {"x": x,
            "wq_words": wq_words, "wq_scales": wq_scales,
            "wk_words": wk_words, "wk_scales": wk_scales,
            "wv_words": wv_words, "wv_scales": wv_scales,
            "q_norm_w": q_norm_w,
            "k_norm_w": k_norm_w}


def reference(x, wq_words, wq_scales, wk_words, wk_scales, wv_words, wv_scales, q_norm_w, k_norm_w):
    xq = mxq(f64(x), 2, "e5m2")
    q = (xq @ unpack4(wq_words, wq_scales)).reshape(B, T, H, DH)
    k = (xq @ unpack4(wk_words, wk_scales)).reshape(B, T, KV, DH)
    v = (xq @ unpack4(wv_words, wv_scales)).reshape(B, T, KV, DH)
    return rope(rms_norm(q, f64(q_norm_w))), rope(rms_norm(k, f64(k_norm_w))), v

@@ -1,0 +1,256 @@
+import math
+from contextlib import ExitStack
+
+import concourse.mybir as mybir
+from concourse.masks import make_identity
+
+F32 = mybir.dt.float32
+BF16 = mybir.dt.bfloat16
+I32 = mybir.dt.int32
+U32 = mybir.dt.uint32
+U8 = mybir.dt.uint8
+E5X4 = mybir.dt.float8_e5m2_x4
+E2X4 = mybir.dt.float4_e2m1fn_x4
+ALU = mybir.AluOpType
+ACT = mybir.ActivationFunctionType
+
+P = 128
+TOK = 512
+D = 2048
+DH = 128
+HALF = 64
+PASSES = 4
+NB = 512
+THETA = 1000000.0
+EPS = 1e-6
+LAG = 3
+
+FLOPS = 2 * TOK * D * 3072
+
+
+def tile_qwen3attention_pa_kernel(
+    tc, x, wq_words, wq_scales, wk_words, wk_scales, wv_words, wv_scales, q_norm_w, k_norm_w, out_0, out_1, out_2
+):
+    nc = tc.nc
+    x_flat = x.flatten_outer_dims()
+    q_flat = out_0.rearrange("b t h d -> (b t) (h d)")
+    k_flat = out_1.rearrange("b t h d -> (b t) (h d)")
+    v_flat = out_2.rearrange("b t h d -> (b t) (h d)")
+    groups = [(wq_words, wq_scales, NB * j, q_flat, NB * j) for j in range(4)]
+    groups.append((wk_words, wk_scales, 0, k_flat, 0))
+    groups.append((wv_words, wv_scales, 0, v_flat, 0))
+
+    with ExitStack() as ctx:
+        const = ctx.enter_context(tc.tile_pool(name="const", bufs=1))
+        keep = ctx.enter_context(tc.tile_pool(name="keep", bufs=1))
+        work = ctx.enter_context(tc.tile_pool(name="work", bufs=6))
+        small = ctx.enter_context(tc.tile_pool(name="small", bufs=8))
+        outp = ctx.enter_context(tc.tile_pool(name="outp", bufs=12))
+        psum = ctx.enter_context(tc.psum_pool(name="psum", bufs=8))
+
+        tcol = const.tile([P, 2], F32, name="tcol")
+        nc.gpsimd.iota(tcol[:], pattern=[[P, 2]], base=0, channel_multiplier=1, allow_small_or_imprecise_dtypes=True)
+        ident = const.tile([P, P], F32, name="ident")
+        make_identity(nc, ident[:])
+        wz = const.tile([P, 2 * DH], BF16, name="wz")
+        nc.vector.memset(wz[:], 0.0)
+        nc.scalar.dma_start(out=wz[0:1, 0:DH], in_=q_norm_w.rearrange("(o d) -> o d", o=1))
+        nc.scalar.dma_start(out=wz[0:1, DH : 2 * DH], in_=k_norm_w.rearrange("(o d) -> o d", o=1))
+
+        planes = []
+        words = []
+        for j in range(6):
+            pl = keep.tile([P, PASSES, NB], U8, name="plane%d" % j, align_bytes=64)
+            wt = keep.tile([P, PASSES, 2 * NB], U8, name="words%d" % j, align_bytes=64)
+            planes.append(pl)
+            words.append(wt)
+        nc.vector.memset(planes[0][:].bitcast(I32), 0)
+        for j in range(1, 6):
+            nc.gpsimd.memset(planes[j][:].bitcast(F32), 0.0)
+
+        zcol = const.tile([P, 1], F32, name="zcol")
+        nc.vector.memset(zcol[:], 0.0)
+        warm = const.tile([P, 1], F32, name="warm")
+        nc.scalar.activation(out=warm[:], in_=zcol[:], func=ACT.Sin)
+
+        ones = const.tile([P, P], BF16, name="ones")
+        nc.vector.memset(ones[:], 1.0)
+
+        xs = []
+        for c in range(8):
+            xs.append(keep.tile([P, 1024], BF16, name="xs%d" % c))
+
+        def load_x(c):
+            mt, hf = c // 2, c % 2
+            nc.sync.dma_start(out=xs[c][:], in_=x_flat[P * mt : P * (mt + 1), 1024 * hf : 1024 * (hf + 1)])
+
+        def load_w(j):
+            wd, sd, c0 = groups[j][0], groups[j][1], groups[j][2]
+            for q in range(4):
+                nc.sync.dma_start(
+                    out=planes[j][32 * q : 32 * q + 4, :, :].bitcast(I32),
+                    in_=sd[:, 4 * q : 4 * q + 4, c0 : c0 + NB].rearrange("g r n -> r g n").bitcast(I32),
+                )
+            nc.sync.dma_start(
+                out=words[j][:].bitcast(I32),
+                in_=wd[:, :, 2 * c0 : 2 * (c0 + NB)].rearrange("g p n -> p g n").bitcast(I32),
+            )
+
+        for c in range(4):
+            load_x(c)
+        load_w(0)
+        for c in range(4, 8):
+            load_x(c)
+        for j in range(1, 6):
+            load_w(j)
+
+        rho = THETA ** (-1.0 / HALF)
+        freq = const.tile([P, HALF], F32, name="freq")
+        nc.vector.memset(freq[:, 0:1], 1.0)
+        w = 1
+        while w < HALF:
+            nc.vector.tensor_scalar(out=freq[:, w : 2 * w], in0=freq[:, 0:w], scalar1=rho**w, scalar2=None, op0=ALU.mult)
+            w = 2 * w
+        turns = const.tile([P, 2, 3, HALF], F32, name="turns")
+        for tt in range(2):
+            nc.vector.tensor_scalar(
+                out=turns[:, tt, 0, :], in0=freq[:], scalar1=tcol[:, tt : tt + 1], scalar2=0.5 / math.pi,
+                op0=ALU.mult, op1=ALU.mult,
+            )
+        nc.vector.tensor_scalar(out=turns[:, :, 1, :], in0=turns[:, :, 0, :], scalar1=0.5, scalar2=None, op0=ALU.add)
+        nc.vector.tensor_scalar(out=turns[:, :, 2, :], in0=turns[:, :, 0, :], scalar1=0.25, scalar2=None, op0=ALU.add)
+        turns_f = turns[:].rearrange("p a b d -> p (a b d)")
+        whole = const.tile([P, 6 * HALF], I32, name="whole")
+        nc.vector.tensor_copy(out=whole[:], in_=turns_f)
+        frac = const.tile([P, 6 * HALF], F32, name="frac")
+        nc.vector.tensor_tensor(out=frac[:], in0=turns_f, in1=whole[:], op=ALU.subtract)
+        nfrac = const.tile([P, 6 * HALF], F32, name="nfrac")
+        nc.vector.scalar_tensor_tensor(out=nfrac[:], in0=frac[:], scalar=0.5, in1=frac[:], op0=ALU.is_ge, op1=ALU.subtract)
+        trig = const.tile([P, 2, 3, HALF], F32, name="trig")
+        nc.scalar.activation(out=trig[:].rearrange("p a b d -> p (a b d)"), in_=nfrac[:], func=ACT.Sin, scale=-2.0 * math.pi)
+
+        grouped = []
+        codes = []
+        xscl = []
+        for c in range(8):
+            grouped.append(keep.tile([P, 2, P, 4], BF16, name="grouped%d" % c, align_bytes=64))
+            codes.append(keep.tile([P, 2 * P], U32, name="codes%d" % c, align_bytes=64))
+            xscl.append(keep.tile([P, 2 * P], U8, name="xscl%d" % c, align_bytes=64))
+
+        def turn_x(c, eng):
+            xw = xs[c][:].bitcast(F32)
+            xt = psum.tile([P, 4, P], F32, name="xt", tag="bank")
+            for g in range(2):
+                for u in range(2):
+                    nc.tensor.transpose(xt[:, 2 * g + u, :], xw[:, 256 * g + u : 256 * (g + 1) : 2], ident[:])
+            src = xt[:].rearrange("p (g u) r -> p g r u", u=2)
+            if eng == 0:
+                nc.vector.tensor_copy(out=grouped[c][:].bitcast(F32), in_=src)
+            else:
+                nc.scalar.copy(out=grouped[c][:].bitcast(F32), in_=src)
+
+        def quant_x(c):
+            nc.vector.quantize_mx(
+                out=codes[c][:].bitcast(E5X4), scales=xscl[c][:], in_=grouped[c][:].rearrange("p g r t -> p (g r t)")
+            )
+
+        turn_x(0, 0)
+        turn_x(1, 0)
+        wps = psum.tile([P, 2 * DH], F32, name="wps", tag="bank")
+        nc.tensor.matmul(out=wps[:], lhsT=ones[:], rhs=wz[:], start=True, stop=True)
+        wsb = const.tile([P, 2, 2, HALF], F32, name="wsb")
+        nc.scalar.copy(out=wsb[:].rearrange("p x s d -> p (x s d)"), in_=wps[:])
+        nc.scalar.activation(out=warm[:], in_=ones[:, 0:1], func=ACT.Abs_reciprocal_sqrt)
+        ctab = const.tile([P, 2, 2, 2, HALF], F32, name="ctab")
+        stab = const.tile([P, 2, 2, 2, HALF], F32, name="stab")
+        for xk in range(2):
+            for tt in range(2):
+                nc.gpsimd.tensor_tensor(
+                    out=ctab[:, tt, xk], in0=wsb[:, xk], in1=trig[:, tt, 2:3, :].to_broadcast([P, 2, HALF]), op=ALU.mult
+                )
+                nc.gpsimd.tensor_tensor(out=stab[:, tt, xk], in0=wsb[:, xk], in1=trig[:, tt, 0:2, :], op=ALU.mult)
+
+        quant_x(0)
+        quant_x(1)
+        turn_x(2, 0)
+        turn_x(3, 0)
+        quant_x(2)
+        quant_x(3)
+
+        def mm(j, mt):
+            acc = psum.tile([P, NB], F32, name="acc", tag="bank")
+            for g in range(PASSES):
+                c = 2 * mt + g // 2
+                cols = slice(P * (g % 2), P * (g % 2 + 1))
+                nc.tensor.matmul_mx(
+                    out=acc[:],
+                    lhsT=codes[c][:, cols].bitcast(E5X4),
+                    lhsT_scale=xscl[c][:, cols],
+                    rhs=words[j][:, g, :].bitcast(E2X4),
+                    rhs_scale=planes[j][:, g, :],
+                    start=(g == 0),
+                    stop=(g == PASSES - 1),
+                )
+            return acc
+
+        def first_half(acc, j, mt):
+            tt = mt % 2
+            xk = 0 if j < 4 else 1
+            ss = small.tile([P, 4], F32, name="ss")
+            for h in range(4):
+                junk = work.tile([P, DH], F32, name="junk")
+                nc.scalar.activation(
+                    out=junk[:], in_=acc[:, DH * h : DH * (h + 1)], func=ACT.Square, accum_out=ss[:, h : h + 1]
+                )
+            a3 = acc[:].rearrange("p (h d) -> p h d", h=4)
+            m1 = work.tile([P, 4, DH], F32, name="m1")
+            m2 = work.tile([P, 4, DH], F32, name="m2")
+            nc.vector.tensor_tensor(
+                out=m1[:], in0=a3,
+                in1=ctab[:, tt, xk].rearrange("p s d -> p (s d)").unsqueeze(1).to_broadcast([P, 4, DH]),
+                op=ALU.mult,
+            )
+            nc.vector.tensor_tensor(
+                out=m2[:, :, 0:HALF], in0=a3[:, :, HALF:DH],
+                in1=stab[:, tt, xk, 1:2, :].to_broadcast([P, 4, HALF]), op=ALU.mult,
+            )
+            nc.vector.tensor_tensor(
+                out=m2[:, :, HALF:DH], in0=a3[:, :, 0:HALF],
+                in1=stab[:, tt, xk, 0:1, :].to_broadcast([P, 4, HALF]), op=ALU.mult,
+            )
+            sm = work.tile([P, 4, DH], F32, name="sm")
+            nc.gpsimd.tensor_tensor(out=sm[:], in0=m1[:], in1=m2[:], op=ALU.add)
+            rr = small.tile([P, 4], F32, name="rr")
+            nc.scalar.activation(out=rr[:], in_=ss[:], func=ACT.Abs_reciprocal_sqrt, scale=1.0 / DH, bias=EPS)
+            return (sm, rr, j, mt)
+
+        def second_half(held):
+            sm, rr, j, mt = held
+            o = outp.tile([P, NB], F32, name="o")
+            for h in range(4):
+                nc.scalar.activation(out=o[:, DH * h : DH * (h + 1)], in_=sm[:, h, :], func=ACT.Copy, scale=rr[:, h : h + 1])
+            dst, d0 = groups[j][3], groups[j][4]
+            nc.sync.dma_start(out=dst[P * mt : P * (mt + 1), d0 : d0 + NB], in_=o[:])
+
+        banks = [(j, mt) for j in range(6) for mt in range(4)]
+        held = []
+        done = 0
+        for j, mt in banks:
+            acc = mm(j, mt)
+            if j == 0 and mt < 2:
+                turn_x(2 * mt + 4, 0)
+                turn_x(2 * mt + 5, 1)
+                quant_x(2 * mt + 4)
+                quant_x(2 * mt + 5)
+            if j < 5:
+                held.append(first_half(acc, j, mt))
+            else:
+                o = outp.tile([P, NB], F32, name="o")
+                nc.vector.tensor_copy(out=o[:], in_=acc[:])
+                nc.sync.dma_start(out=v_flat[P * mt : P * (mt + 1), :], in_=o[:])
+            if len(held) - done > LAG or (j == 5 and done < len(held)):
+                second_half(held[done])
+                done += 1
+        while done < len(held):
+            second_half(held[done])
+            done += 1

@@ -104,6 +104,9 @@ def tile_qwen3attention_pa_kernel(
         for j in range(1, 6):
             load_w(j)
 
+        wps = psum.tile([P, 2 * DH], F32, name="wps", tag="bank")
+        nc.tensor.matmul(out=wps[:], lhsT=ones[:], rhs=wz[:], start=True, stop=True)
+
         rho = THETA ** (-1.0 / HALF)
         freq = const.tile([P, HALF], F32, name="freq")
         nc.vector.memset(freq[:, 0:1], 1.0)
@@ -111,23 +114,36 @@ def tile_qwen3attention_pa_kernel(
         while w < HALF:
             nc.vector.tensor_scalar(out=freq[:, w : 2 * w], in0=freq[:, 0:w], scalar1=rho**w, scalar2=None, op0=ALU.mult)
             w = 2 * w
-        turns = const.tile([P, 2, 3, HALF], F32, name="turns")
+        turns = const.tile([P, 2, 4, HALF], F32, name="turns")
         for tt in range(2):
             nc.vector.tensor_scalar(
-                out=turns[:, tt, 0, :], in0=freq[:], scalar1=tcol[:, tt : tt + 1], scalar2=0.5 / math.pi,
+                out=turns[:, tt, 2, :], in0=freq[:], scalar1=tcol[:, tt : tt + 1], scalar2=0.5 / math.pi,
                 op0=ALU.mult, op1=ALU.mult,
             )
-        nc.vector.tensor_scalar(out=turns[:, :, 1, :], in0=turns[:, :, 0, :], scalar1=0.5, scalar2=None, op0=ALU.add)
-        nc.vector.tensor_scalar(out=turns[:, :, 2, :], in0=turns[:, :, 0, :], scalar1=0.25, scalar2=None, op0=ALU.add)
+        nc.vector.tensor_scalar(out=turns[:, :, 3, :], in0=turns[:, :, 2, :], scalar1=0.5, scalar2=None, op0=ALU.add)
+        nc.vector.tensor_scalar(
+            out=turns[:, :, 0:2, :], in0=turns[:, :, 2:3, :].to_broadcast([P, 2, 2, HALF]), scalar1=0.25, scalar2=None,
+            op0=ALU.add,
+        )
         turns_f = turns[:].rearrange("p a b d -> p (a b d)")
-        whole = const.tile([P, 6 * HALF], I32, name="whole")
+        whole = const.tile([P, 8 * HALF], I32, name="whole")
         nc.vector.tensor_copy(out=whole[:], in_=turns_f)
-        frac = const.tile([P, 6 * HALF], F32, name="frac")
+        frac = const.tile([P, 8 * HALF], F32, name="frac")
         nc.vector.tensor_tensor(out=frac[:], in0=turns_f, in1=whole[:], op=ALU.subtract)
-        nfrac = const.tile([P, 6 * HALF], F32, name="nfrac")
+        nfrac = const.tile([P, 8 * HALF], F32, name="nfrac")
         nc.vector.scalar_tensor_tensor(out=nfrac[:], in0=frac[:], scalar=0.5, in1=frac[:], op0=ALU.is_ge, op1=ALU.subtract)
-        trig = const.tile([P, 2, 3, HALF], F32, name="trig")
+        trig = const.tile([P, 2, 2, DH], F32, name="trig")
         nc.scalar.activation(out=trig[:].rearrange("p a b d -> p (a b d)"), in_=nfrac[:], func=ACT.Sin, scale=-2.0 * math.pi)
+        nc.scalar.activation(out=warm[:], in_=trig[:, 0, 0, 0:1], func=ACT.Abs_reciprocal_sqrt)
+        tab = const.tile([P, 2, 2, 2, DH], F32, name="tab")
+
+        def make_tab(xk):
+            nc.vector.tensor_tensor(
+                out=tab[:, :, xk], in0=trig[:],
+                in1=wps[:, DH * xk : DH * (xk + 1)].unsqueeze(1).unsqueeze(1).to_broadcast([P, 2, 2, DH]), op=ALU.mult,
+            )
+
+        make_tab(0)
 
         grouped = []
         codes = []
@@ -156,26 +172,13 @@ def tile_qwen3attention_pa_kernel(
 
         turn_x(0, 0)
         turn_x(1, 0)
-        wps = psum.tile([P, 2 * DH], F32, name="wps", tag="bank")
-        nc.tensor.matmul(out=wps[:], lhsT=ones[:], rhs=wz[:], start=True, stop=True)
-        wsb = const.tile([P, 2, 2, HALF], F32, name="wsb")
-        nc.scalar.copy(out=wsb[:].rearrange("p x s d -> p (x s d)"), in_=wps[:])
-        nc.scalar.activation(out=warm[:], in_=ones[:, 0:1], func=ACT.Abs_reciprocal_sqrt)
-        ctab = const.tile([P, 2, 2, 2, HALF], F32, name="ctab")
-        stab = const.tile([P, 2, 2, 2, HALF], F32, name="stab")
-        for xk in range(2):
-            for tt in range(2):
-                nc.gpsimd.tensor_tensor(
-                    out=ctab[:, tt, xk], in0=wsb[:, xk], in1=trig[:, tt, 2:3, :].to_broadcast([P, 2, HALF]), op=ALU.mult
-                )
-                nc.gpsimd.tensor_tensor(out=stab[:, tt, xk], in0=wsb[:, xk], in1=trig[:, tt, 0:2, :], op=ALU.mult)
-
         quant_x(0)
         quant_x(1)
         turn_x(2, 0)
         turn_x(3, 0)
         quant_x(2)
         quant_x(3)
+        make_tab(1)
 
         def mm(j, mt):
             acc = psum.tile([P, NB], F32, name="acc", tag="bank")
@@ -203,23 +206,17 @@ def tile_qwen3attention_pa_kernel(
                     out=junk[:], in_=acc[:, DH * h : DH * (h + 1)], func=ACT.Square, accum_out=ss[:, h : h + 1]
                 )
             a3 = acc[:].rearrange("p (h d) -> p h d", h=4)
-            m1 = work.tile([P, 4, DH], F32, name="m1")
-            m2 = work.tile([P, 4, DH], F32, name="m2")
+            prod = work.tile([P, 2, 4, DH], F32, name="prod")
             nc.vector.tensor_tensor(
-                out=m1[:], in0=a3,
-                in1=ctab[:, tt, xk].rearrange("p s d -> p (s d)").unsqueeze(1).to_broadcast([P, 4, DH]),
+                out=prod[:], in0=a3.unsqueeze(1).to_broadcast([P, 2, 4, DH]),
+                in1=tab[:, tt, xk].unsqueeze(2).to_broadcast([P, 2, 4, DH]),
                 op=ALU.mult,
             )
-            nc.vector.tensor_tensor(
-                out=m2[:, :, 0:HALF], in0=a3[:, :, HALF:DH],
-                in1=stab[:, tt, xk, 1:2, :].to_broadcast([P, 4, HALF]), op=ALU.mult,
-            )
-            nc.vector.tensor_tensor(
-                out=m2[:, :, HALF:DH], in0=a3[:, :, 0:HALF],
-                in1=stab[:, tt, xk, 0:1, :].to_broadcast([P, 4, HALF]), op=ALU.mult,
-            )
+            p5 = prod[:].rearrange("p k h (s d) -> p k h s d", s=2)
             sm = work.tile([P, 4, DH], F32, name="sm")
-            nc.gpsimd.tensor_tensor(out=sm[:], in0=m1[:], in1=m2[:], op=ALU.add)
+            nc.gpsimd.tensor_tensor(
+                out=sm[:].rearrange("p h (s d) -> p h s d", s=2), in0=p5[:, 0], in1=p5[:, 1, :, ::-1, :], op=ALU.add
+            )
             rr = small.tile([P, 4], F32, name="rr")
             nc.scalar.activation(out=rr[:], in_=ss[:], func=ACT.Abs_reciprocal_sqrt, scale=1.0 / DH, bias=EPS)
             return (sm, rr, j, mt)

@@ -23,7 +23,7 @@ PASSES = 4
 NB = 512
 THETA = 1000000.0
 EPS = 1e-6
-LAG = 3
+LAG = 4
 
 FLOPS = 2 * TOK * D * 3072
 
@@ -218,36 +218,39 @@ def tile_qwen3attention_pa_kernel(
                 out=sm[:].rearrange("p h (s d) -> p h s d", s=2), in0=p5[:, 0], in1=p5[:, 1, :, ::-1, :], op=ALU.add
             )
             rr = small.tile([P, 4], F32, name="rr")
+            return (sm, ss, rr, j, mt)
+
+        def inv_rms(held):
+            sm, ss, rr, j, mt = held
             nc.scalar.activation(out=rr[:], in_=ss[:], func=ACT.Abs_reciprocal_sqrt, scale=1.0 / DH, bias=EPS)
-            return (sm, rr, j, mt)
 
         def second_half(held):
-            sm, rr, j, mt = held
+            sm, ss, rr, j, mt = held
             o = outp.tile([P, NB], F32, name="o")
             for h in range(4):
                 nc.scalar.activation(out=o[:, DH * h : DH * (h + 1)], in_=sm[:, h, :], func=ACT.Copy, scale=rr[:, h : h + 1])
             dst, d0 = groups[j][3], groups[j][4]
             nc.sync.dma_start(out=dst[P * mt : P * (mt + 1), d0 : d0 + NB], in_=o[:])
 
+        ctx.enter_context(tc.manual_schedule(engines={mybir.EngineType.Activation}))
         banks = [(j, mt) for j in range(6) for mt in range(4)]
         held = []
-        done = 0
-        for j, mt in banks:
-            acc = mm(j, mt)
-            if j == 0 and mt < 2:
-                turn_x(2 * mt + 4, 0)
-                turn_x(2 * mt + 5, 1)
-                quant_x(2 * mt + 4)
-                quant_x(2 * mt + 5)
-            if j < 5:
-                held.append(first_half(acc, j, mt))
-            else:
-                o = outp.tile([P, NB], F32, name="o")
-                nc.vector.tensor_copy(out=o[:], in_=acc[:])
-                nc.sync.dma_start(out=v_flat[P * mt : P * (mt + 1), :], in_=o[:])
-            if len(held) - done > LAG or (j == 5 and done < len(held)):
-                second_half(held[done])
-                done += 1
-        while done < len(held):
-            second_half(held[done])
-            done += 1
+        for n in range(len(banks) + LAG):
+            if n < len(banks):
+                j, mt = banks[n]
+                acc = mm(j, mt)
+                if j < 5:
+                    held.append(first_half(acc, j, mt))
+                else:
+                    o = outp.tile([P, NB], F32, name="o")
+                    nc.vector.tensor_copy(out=o[:], in_=acc[:])
+                    nc.sync.dma_start(out=v_flat[P * mt : P * (mt + 1), :], in_=o[:])
+                if j == 0 and mt < 2:
+                    turn_x(2 * mt + 4, 0)
+                    turn_x(2 * mt + 5, 1)
+                    quant_x(2 * mt + 4)
+                    quant_x(2 * mt + 5)
+            if 1 <= n <= len(held):
+                inv_rms(held[n - 1])
+            if LAG <= n < len(held) + LAG:
+                second_half(held[n - LAG])

@@ -23,7 +23,6 @@ PASSES = 4
 NB = 512
 THETA = 1000000.0
 EPS = 1e-6
-LAG = 4
 
 FLOPS = 2 * TOK * D * 3072
 
@@ -174,8 +173,8 @@ def tile_qwen3attention_pa_kernel(
         turn_x(1, 0)
         quant_x(0)
         quant_x(1)
-        turn_x(2, 0)
-        turn_x(3, 0)
+        turn_x(2, 1)
+        turn_x(3, 1)
         quant_x(2)
         quant_x(3)
         make_tab(1)
@@ -196,61 +195,52 @@ def tile_qwen3attention_pa_kernel(
                 )
             return acc
 
-        def first_half(acc, j, mt):
-            tt = mt % 2
-            xk = 0 if j < 4 else 1
+        def squares(acc):
             ss = small.tile([P, 4], F32, name="ss")
             for h in range(4):
                 junk = work.tile([P, DH], F32, name="junk")
                 nc.scalar.activation(
                     out=junk[:], in_=acc[:, DH * h : DH * (h + 1)], func=ACT.Square, accum_out=ss[:, h : h + 1]
                 )
-            a3 = acc[:].rearrange("p (h d) -> p h d", h=4)
-            prod = work.tile([P, 2, 4, DH], F32, name="prod")
-            nc.vector.tensor_tensor(
-                out=prod[:], in0=a3.unsqueeze(1).to_broadcast([P, 2, 4, DH]),
-                in1=tab[:, tt, xk].unsqueeze(2).to_broadcast([P, 2, 4, DH]),
-                op=ALU.mult,
-            )
-            p5 = prod[:].rearrange("p k h (s d) -> p k h s d", s=2)
-            sm = work.tile([P, 4, DH], F32, name="sm")
-            nc.gpsimd.tensor_tensor(
-                out=sm[:].rearrange("p h (s d) -> p h s d", s=2), in0=p5[:, 0], in1=p5[:, 1, :, ::-1, :], op=ALU.add
-            )
+            return ss
+
+        def norm_rope_store(acc, ss, j, mt):
+            tt = mt % 2
+            xk = 0 if j < 4 else 1
             rr = small.tile([P, 4], F32, name="rr")
-            return (sm, ss, rr, j, mt)
-
-        def inv_rms(held):
-            sm, ss, rr, j, mt = held
             nc.scalar.activation(out=rr[:], in_=ss[:], func=ACT.Abs_reciprocal_sqrt, scale=1.0 / DH, bias=EPS)
-
-        def second_half(held):
-            sm, ss, rr, j, mt = held
-            o = outp.tile([P, NB], F32, name="o")
+            prod = work.tile([P, 2, 4, DH], F32, name="prod")
             for h in range(4):
-                nc.scalar.activation(out=o[:, DH * h : DH * (h + 1)], in_=sm[:, h, :], func=ACT.Copy, scale=rr[:, h : h + 1])
+                nc.vector.scalar_tensor_tensor(
+                    out=prod[:, :, h, :], in0=acc[:, DH * h : DH * (h + 1)].unsqueeze(1).to_broadcast([P, 2, DH]),
+                    scalar=rr[:, h : h + 1], in1=tab[:, tt, xk], op0=ALU.mult, op1=ALU.mult,
+                )
+            p5 = prod[:].rearrange("p k h (s d) -> p k h s d", s=2)
+            o = outp.tile([P, NB], F32, name="o")
+            nc.gpsimd.tensor_tensor(
+                out=o[:].rearrange("p (h s d) -> p h s d", h=4, s=2), in0=p5[:, 0], in1=p5[:, 1, :, ::-1, :], op=ALU.add
+            )
             dst, d0 = groups[j][3], groups[j][4]
             nc.sync.dma_start(out=dst[P * mt : P * (mt + 1), d0 : d0 + NB], in_=o[:])
 
         ctx.enter_context(tc.manual_schedule(engines={mybir.EngineType.Activation}))
         banks = [(j, mt) for j in range(6) for mt in range(4)]
         held = []
-        for n in range(len(banks) + LAG):
+        for n in range(len(banks) + 1):
             if n < len(banks):
                 j, mt = banks[n]
                 acc = mm(j, mt)
                 if j < 5:
-                    held.append(first_half(acc, j, mt))
-                else:
+                    held.append((acc, squares(acc), j, mt))
+            if 1 <= n <= len(held):
+                norm_rope_store(*held[n - 1])
+            if n < len(banks):
+                if j == 5:
                     o = outp.tile([P, NB], F32, name="o")
-                    nc.vector.tensor_copy(out=o[:], in_=acc[:])
+                    nc.scalar.copy(out=o[:], in_=acc[:])
                     nc.sync.dma_start(out=v_flat[P * mt : P * (mt + 1), :], in_=o[:])
                 if j == 0 and mt < 2:
-                    turn_x(2 * mt + 4, 0)
+                    turn_x(2 * mt + 4, 1)
                     turn_x(2 * mt + 5, 1)
                     quant_x(2 * mt + 4)
                     quant_x(2 * mt + 5)
-            if 1 <= n <= len(held):
-                inv_rms(held[n - 1])
-            if LAG <= n < len(held) + LAG:
-                second_half(held[n - LAG])

@@ -217,25 +217,20 @@ def tile_qwen3attention_pa_kernel(
                 )
             p5 = prod[:].rearrange("p k h (s d) -> p k h s d", s=2)
             o = outp.tile([P, NB], F32, name="o")
-            nc.gpsimd.tensor_tensor(
+            adder = nc.vector if mt == 3 else nc.gpsimd
+            adder.tensor_tensor(
                 out=o[:].rearrange("p (h s d) -> p h s d", h=4, s=2), in0=p5[:, 0], in1=p5[:, 1, :, ::-1, :], op=ALU.add
             )
             dst, d0 = groups[j][3], groups[j][4]
             nc.sync.dma_start(out=dst[P * mt : P * (mt + 1), d0 : d0 + NB], in_=o[:])
 
         ctx.enter_context(tc.manual_schedule(engines={mybir.EngineType.Activation}))
-        banks = [(j, mt) for j in range(6) for mt in range(4)]
-        held = []
-        for n in range(len(banks) + 1):
-            if n < len(banks):
-                j, mt = banks[n]
+        for j in range(6):
+            for mt in range(4):
                 acc = mm(j, mt)
                 if j < 5:
-                    held.append((acc, squares(acc), j, mt))
-            if 1 <= n <= len(held):
-                norm_rope_store(*held[n - 1])
-            if n < len(banks):
-                if j == 5:
+                    norm_rope_store(acc, squares(acc), j, mt)
+                else:
                     o = outp.tile([P, NB], F32, name="o")
                     nc.scalar.copy(out=o[:], in_=acc[:])
                     nc.sync.dma_start(out=v_flat[P * mt : P * (mt + 1), :], in_=o[:])

@@ -204,7 +204,7 @@ def tile_qwen3attention_pa_kernel(
                 )
             return ss
 
-        def norm_rope_store(acc, ss, j, mt):
+        def norm_rope(acc, ss, j, mt):
             tt = mt % 2
             xk = 0 if j < 4 else 1
             rr = small.tile([P, 4], F32, name="rr")
@@ -215,25 +215,35 @@ def tile_qwen3attention_pa_kernel(
                     out=prod[:, :, h, :], in0=acc[:, DH * h : DH * (h + 1)].unsqueeze(1).to_broadcast([P, 2, DH]),
                     scalar=rr[:, h : h + 1], in1=tab[:, tt, xk], op0=ALU.mult, op1=ALU.mult,
                 )
+            return prod
+
+        def add_store(adder, prod, j, mt):
             p5 = prod[:].rearrange("p k h (s d) -> p k h s d", s=2)
             o = outp.tile([P, NB], F32, name="o")
-            adder = nc.vector if mt == 3 else nc.gpsimd
             adder.tensor_tensor(
                 out=o[:].rearrange("p (h s d) -> p h s d", h=4, s=2), in0=p5[:, 0], in1=p5[:, 1, :, ::-1, :], op=ALU.add
             )
             dst, d0 = groups[j][3], groups[j][4]
             nc.sync.dma_start(out=dst[P * mt : P * (mt + 1), d0 : d0 + NB], in_=o[:])
 
-        ctx.enter_context(tc.manual_schedule(engines={mybir.EngineType.Activation}))
+        ctx.enter_context(tc.manual_schedule(engines={mybir.EngineType.Activation, mybir.EngineType.DVE}))
+        late = []
         for j in range(6):
             for mt in range(4):
                 acc = mm(j, mt)
                 if j < 5:
-                    norm_rope_store(acc, squares(acc), j, mt)
-                else:
+                    prod = norm_rope(acc, squares(acc), j, mt)
+                for args in late:
+                    add_store(nc.vector, *args)
+                late.clear()
+                if j == 5:
                     o = outp.tile([P, NB], F32, name="o")
                     nc.scalar.copy(out=o[:], in_=acc[:])
                     nc.sync.dma_start(out=v_flat[P * mt : P * (mt + 1), :], in_=o[:])
+                elif mt == 3:
+                    late.append((prod, j, mt))
+                else:
+                    add_store(nc.gpsimd, prod, j, mt)
                 if j == 0 and mt < 2:
                     turn_x(2 * mt + 4, 1)
                     turn_x(2 * mt + 5, 1)

@@ -240,7 +240,7 @@ def tile_qwen3attention_pa_kernel(
                     o = outp.tile([P, NB], F32, name="o")
                     nc.scalar.copy(out=o[:], in_=acc[:])
                     nc.sync.dma_start(out=v_flat[P * mt : P * (mt + 1), :], in_=o[:])
-                elif mt == 3:
+                elif (4 * j + mt) % 5 == 4:
                     late.append((prod, j, mt))
                 else:
                     add_store(nc.gpsimd, prod, j, mt)

@@ -240,7 +240,7 @@ def tile_qwen3attention_pa_kernel(
                     o = outp.tile([P, NB], F32, name="o")
                     nc.scalar.copy(out=o[:], in_=acc[:])
                     nc.sync.dma_start(out=v_flat[P * mt : P * (mt + 1), :], in_=o[:])
-                elif (4 * j + mt) % 5 == 4:
+                elif (4 * j + mt) % 10 == 9:
                     late.append((prod, j, mt))
                 else:
                     add_store(nc.gpsimd, prod, j, mt)

@@ -49,8 +49,14 @@ def tile_qwen3attention_pa_kernel(
 
         tcol = const.tile([P, 2], F32, name="tcol")
         nc.gpsimd.iota(tcol[:], pattern=[[P, 2]], base=0, channel_multiplier=1, allow_small_or_imprecise_dtypes=True)
+        step = const.tile([P, HALF], F32, name="step")
+        nc.gpsimd.memset(step[:], 1.0)
+        zero = const.tile([P, HALF], F32, name="zero")
+        nc.gpsimd.memset(zero[:], 0.0)
         ident = const.tile([P, P], F32, name="ident")
         make_identity(nc, ident[:])
+        neg_ones = const.tile([P, P], BF16, name="neg_ones")
+        nc.gpsimd.memset(neg_ones[:], -1.0)
         wz = const.tile([P, 2 * DH], BF16, name="wz")
         nc.vector.memset(wz[:], 0.0)
         nc.scalar.dma_start(out=wz[0:1, 0:DH], in_=q_norm_w.rearrange("(o d) -> o d", o=1))
@@ -103,43 +109,43 @@ def tile_qwen3attention_pa_kernel(
         for j in range(1, 6):
             load_w(j)
 
-        wps = psum.tile([P, 2 * DH], F32, name="wps", tag="bank")
-        nc.tensor.matmul(out=wps[:], lhsT=ones[:], rhs=wz[:], start=True, stop=True)
+        wps = psum.tile([P, 2, 2, DH], F32, name="wps", tag="bank")
+        for xk in range(2):
+            wrow = wz[:, DH * xk : DH * (xk + 1)]
+            nc.tensor.matmul(out=wps[:, xk, 0, :], lhsT=ones[:], rhs=wrow, start=True, stop=True)
+            nc.tensor.matmul(out=wps[:, xk, 1, 0:HALF], lhsT=ones[:], rhs=wrow[:, 0:HALF], start=True, stop=True)
+            nc.tensor.matmul(out=wps[:, xk, 1, HALF:DH], lhsT=neg_ones[:], rhs=wrow[:, HALF:DH], start=True, stop=True)
 
         rho = THETA ** (-1.0 / HALF)
+        nc.vector.tensor_scalar(out=step[:, 1:HALF], in0=step[:, 1:HALF], scalar1=rho, scalar2=None, op0=ALU.mult)
         freq = const.tile([P, HALF], F32, name="freq")
-        nc.vector.memset(freq[:, 0:1], 1.0)
-        w = 1
-        while w < HALF:
-            nc.vector.tensor_scalar(out=freq[:, w : 2 * w], in0=freq[:, 0:w], scalar1=rho**w, scalar2=None, op0=ALU.mult)
-            w = 2 * w
-        turns = const.tile([P, 2, 4, HALF], F32, name="turns")
-        for tt in range(2):
-            nc.vector.tensor_scalar(
-                out=turns[:, tt, 2, :], in0=freq[:], scalar1=tcol[:, tt : tt + 1], scalar2=0.5 / math.pi,
-                op0=ALU.mult, op1=ALU.mult,
-            )
-        nc.vector.tensor_scalar(out=turns[:, :, 3, :], in0=turns[:, :, 2, :], scalar1=0.5, scalar2=None, op0=ALU.add)
-        nc.vector.tensor_scalar(
-            out=turns[:, :, 0:2, :], in0=turns[:, :, 2:3, :].to_broadcast([P, 2, 2, HALF]), scalar1=0.25, scalar2=None,
-            op0=ALU.add,
+        nc.vector.tensor_tensor_scan(
+            out=freq[:], data0=step[:], data1=zero[:], initial=0.5 / math.pi, op0=ALU.mult, op1=ALU.add
         )
+        turns = const.tile([P, 2, 2, HALF], F32, name="turns")
+        nc.vector.tensor_tensor(
+            out=turns[:, :, 1, :], in0=freq[:].unsqueeze(1).to_broadcast([P, 2, HALF]),
+            in1=tcol[:].unsqueeze(2).to_broadcast([P, 2, HALF]), op=ALU.mult,
+        )
+        nc.vector.tensor_scalar(out=turns[:, :, 0, :], in0=turns[:, :, 1, :], scalar1=0.25, scalar2=None, op0=ALU.add)
         turns_f = turns[:].rearrange("p a b d -> p (a b d)")
-        whole = const.tile([P, 8 * HALF], I32, name="whole")
+        whole = const.tile([P, 4 * HALF], I32, name="whole")
         nc.vector.tensor_copy(out=whole[:], in_=turns_f)
-        frac = const.tile([P, 8 * HALF], F32, name="frac")
+        frac = const.tile([P, 4 * HALF], F32, name="frac")
         nc.vector.tensor_tensor(out=frac[:], in0=turns_f, in1=whole[:], op=ALU.subtract)
-        nfrac = const.tile([P, 8 * HALF], F32, name="nfrac")
+        nfrac = const.tile([P, 4 * HALF], F32, name="nfrac")
         nc.vector.scalar_tensor_tensor(out=nfrac[:], in0=frac[:], scalar=0.5, in1=frac[:], op0=ALU.is_ge, op1=ALU.subtract)
-        trig = const.tile([P, 2, 2, DH], F32, name="trig")
+        trig = const.tile([P, 2, 2, HALF], F32, name="trig")
         nc.scalar.activation(out=trig[:].rearrange("p a b d -> p (a b d)"), in_=nfrac[:], func=ACT.Sin, scale=-2.0 * math.pi)
         nc.scalar.activation(out=warm[:], in_=trig[:, 0, 0, 0:1], func=ACT.Abs_reciprocal_sqrt)
         tab = const.tile([P, 2, 2, 2, DH], F32, name="tab")
 
         def make_tab(xk):
             nc.vector.tensor_tensor(
-                out=tab[:, :, xk], in0=trig[:],
-                in1=wps[:, DH * xk : DH * (xk + 1)].unsqueeze(1).unsqueeze(1).to_broadcast([P, 2, 2, DH]), op=ALU.mult,
+                out=tab[:, xk].rearrange("p t k (s d) -> p t k s d", s=2),
+                in0=trig[:].unsqueeze(3).to_broadcast([P, 2, 2, 2, HALF]),
+                in1=wps[:, xk].rearrange("p k (s d) -> p k s d", s=2).unsqueeze(1).to_broadcast([P, 2, 2, 2, HALF]),
+                op=ALU.mult,
             )
 
         make_tab(0)
@@ -213,7 +219,7 @@ def tile_qwen3attention_pa_kernel(
             for h in range(4):
                 nc.vector.scalar_tensor_tensor(
                     out=prod[:, :, h, :], in0=acc[:, DH * h : DH * (h + 1)].unsqueeze(1).to_broadcast([P, 2, DH]),
-                    scalar=rr[:, h : h + 1], in1=tab[:, tt, xk], op0=ALU.mult, op1=ALU.mult,
+                    scalar=rr[:, h : h + 1], in1=tab[:, xk, tt], op0=ALU.mult, op1=ALU.mult,
                 )
             return prod
 

@@ -78,8 +78,9 @@ def tile_qwen3attention_pa_kernel(
         warm = const.tile([P, 1], F32, name="warm")
         nc.scalar.activation(out=warm[:], in_=zcol[:], func=ACT.Sin)
 
-        ones = const.tile([P, P], BF16, name="ones")
-        nc.vector.memset(ones[:], 1.0)
+        wide_ones = const.tile([P, NB], BF16, name="wide_ones")
+        nc.vector.memset(wide_ones[:], 1.0)
+        ones = wide_ones[:, 0:P]
 
         xs = []
         for c in range(8):
@@ -108,13 +109,6 @@ def tile_qwen3attention_pa_kernel(
             load_x(c)
         for j in range(1, 6):
             load_w(j)
-
-        wps = psum.tile([P, 2, 2, DH], F32, name="wps", tag="bank")
-        for xk in range(2):
-            wrow = wz[:, DH * xk : DH * (xk + 1)]
-            nc.tensor.matmul(out=wps[:, xk, 0, :], lhsT=ones[:], rhs=wrow, start=True, stop=True)
-            nc.tensor.matmul(out=wps[:, xk, 1, 0:HALF], lhsT=ones[:], rhs=wrow[:, 0:HALF], start=True, stop=True)
-            nc.tensor.matmul(out=wps[:, xk, 1, HALF:DH], lhsT=neg_ones[:], rhs=wrow[:, HALF:DH], start=True, stop=True)
 
         rho = THETA ** (-1.0 / HALF)
         nc.vector.tensor_scalar(out=step[:, 1:HALF], in0=step[:, 1:HALF], scalar1=rho, scalar2=None, op0=ALU.mult)
@@ -148,7 +142,6 @@ def tile_qwen3attention_pa_kernel(
                 op=ALU.mult,
             )
 
-        make_tab(0)
 
         grouped = []
         codes = []
@@ -175,14 +168,32 @@ def tile_qwen3attention_pa_kernel(
                 out=codes[c][:].bitcast(E5X4), scales=xscl[c][:], in_=grouped[c][:].rearrange("p g r t -> p (g r t)")
             )
 
-        turn_x(0, 0)
-        turn_x(1, 0)
-        quant_x(0)
-        quant_x(1)
-        turn_x(2, 1)
-        turn_x(3, 1)
-        quant_x(2)
-        quant_x(3)
+        idle = psum.tile([P, NB], F32, name="idle", tag="bank")
+
+        def spin(n):
+            for i in range(n):
+                nc.tensor.matmul(out=idle[:], lhsT=ones, rhs=wide_ones[:], start=True, stop=True)
+
+        with tc.manual_schedule(engines={mybir.EngineType.PE}):
+            spin(5)
+            turn_x(0, 0)
+            turn_x(1, 0)
+            quant_x(0)
+            quant_x(1)
+            spin(1)
+            turn_x(2, 1)
+            turn_x(3, 1)
+            quant_x(2)
+            quant_x(3)
+            wps = psum.tile([P, 2, 2, DH], F32, name="wps", tag="bank")
+            for xk in range(2):
+                wrow = wz[:, DH * xk : DH * (xk + 1)]
+                nc.tensor.matmul(out=wps[:, xk, 0, :], lhsT=ones, rhs=wrow, start=True, stop=True)
+                nc.tensor.matmul(out=wps[:, xk, 1, 0:HALF], lhsT=ones, rhs=wrow[:, 0:HALF], start=True, stop=True)
+                nc.tensor.matmul(out=wps[:, xk, 1, HALF:DH], lhsT=neg_ones[:], rhs=wrow[:, HALF:DH], start=True, stop=True)
+
+            spin(1)
+        make_tab(0)
         make_tab(1)
 
         def mm(j, mt):

@@ -243,7 +243,9 @@ def tile_qwen3attention_pa_kernel(
             dst, d0 = groups[j][3], groups[j][4]
             nc.sync.dma_start(out=dst[P * mt : P * (mt + 1), d0 : d0 + NB], in_=o[:])
 
-        ctx.enter_context(tc.manual_schedule(engines={mybir.EngineType.Activation, mybir.EngineType.DVE}))
+        ctx.enter_context(
+            tc.manual_schedule(engines={mybir.EngineType.PE, mybir.EngineType.Activation, mybir.EngineType.DVE})
+        )
         late = []
         for j in range(6):
             for mt in range(4):
@@ -266,3 +268,5 @@ def tile_qwen3attention_pa_kernel(
                     turn_x(2 * mt + 5, 1)
                     quant_x(2 * mt + 4)
                     quant_x(2 * mt + 5)
+                if j == 0 and mt in (1, 2):
+                    spin(6 - 2 * mt)

@@ -192,7 +192,7 @@ def tile_qwen3attention_pa_kernel(
                 nc.tensor.matmul(out=wps[:, xk, 1, 0:HALF], lhsT=ones, rhs=wrow[:, 0:HALF], start=True, stop=True)
                 nc.tensor.matmul(out=wps[:, xk, 1, HALF:DH], lhsT=neg_ones[:], rhs=wrow[:, HALF:DH], start=True, stop=True)
 
-            spin(1)
+            spin(4)
         make_tab(0)
         make_tab(1)
 

import math
from contextlib import ExitStack

import concourse.mybir as mybir
from concourse.masks import make_identity

F32 = mybir.dt.float32
BF16 = mybir.dt.bfloat16
I32 = mybir.dt.int32
U32 = mybir.dt.uint32
U8 = mybir.dt.uint8
E5X4 = mybir.dt.float8_e5m2_x4
E2X4 = mybir.dt.float4_e2m1fn_x4
ALU = mybir.AluOpType
ACT = mybir.ActivationFunctionType

P = 128
TOK = 512
D = 2048
DH = 128
HALF = 64
PASSES = 4
NB = 512
THETA = 1000000.0
EPS = 1e-6

FLOPS = 2 * TOK * D * 3072


def tile_qwen3attention_pa_kernel(
    tc, x, wq_words, wq_scales, wk_words, wk_scales, wv_words, wv_scales, q_norm_w, k_norm_w, out_0, out_1, out_2
):
    nc = tc.nc
    x_flat = x.flatten_outer_dims()
    q_flat = out_0.rearrange("b t h d -> (b t) (h d)")
    k_flat = out_1.rearrange("b t h d -> (b t) (h d)")
    v_flat = out_2.rearrange("b t h d -> (b t) (h d)")
    groups = [(wq_words, wq_scales, NB * j, q_flat, NB * j) for j in range(4)]
    groups.append((wk_words, wk_scales, 0, k_flat, 0))
    groups.append((wv_words, wv_scales, 0, v_flat, 0))

    with ExitStack() as ctx:
        const = ctx.enter_context(tc.tile_pool(name="const", bufs=1))
        keep = ctx.enter_context(tc.tile_pool(name="keep", bufs=1))
        work = ctx.enter_context(tc.tile_pool(name="work", bufs=6))
        small = ctx.enter_context(tc.tile_pool(name="small", bufs=8))
        outp = ctx.enter_context(tc.tile_pool(name="outp", bufs=12))
        psum = ctx.enter_context(tc.psum_pool(name="psum", bufs=8))

        tcol = const.tile([P, 2], F32, name="tcol")
        nc.gpsimd.iota(tcol[:], pattern=[[P, 2]], base=0, channel_multiplier=1, allow_small_or_imprecise_dtypes=True)
        step = const.tile([P, HALF], F32, name="step")
        nc.gpsimd.memset(step[:], 1.0)
        zero = const.tile([P, HALF], F32, name="zero")
        nc.gpsimd.memset(zero[:], 0.0)
        ident = const.tile([P, P], F32, name="ident")
        make_identity(nc, ident[:])
        neg_ones = const.tile([P, P], BF16, name="neg_ones")
        nc.gpsimd.memset(neg_ones[:], -1.0)
        wz = const.tile([P, 2 * DH], BF16, name="wz")
        nc.vector.memset(wz[:], 0.0)
        nc.scalar.dma_start(out=wz[0:1, 0:DH], in_=q_norm_w.rearrange("(o d) -> o d", o=1))
        nc.scalar.dma_start(out=wz[0:1, DH : 2 * DH], in_=k_norm_w.rearrange("(o d) -> o d", o=1))

        planes = []
        words = []
        for j in range(6):
            pl = keep.tile([P, PASSES, NB], U8, name="plane%d" % j, align_bytes=64)
            wt = keep.tile([P, PASSES, 2 * NB], U8, name="words%d" % j, align_bytes=64)
            planes.append(pl)
            words.append(wt)
        nc.vector.memset(planes[0][:].bitcast(I32), 0)
        for j in range(1, 6):
            nc.gpsimd.memset(planes[j][:].bitcast(F32), 0.0)

        zcol = const.tile([P, 1], F32, name="zcol")
        nc.vector.memset(zcol[:], 0.0)
        warm = const.tile([P, 1], F32, name="warm")
        nc.scalar.activation(out=warm[:], in_=zcol[:], func=ACT.Sin)

        wide_ones = const.tile([P, NB], BF16, name="wide_ones")
        nc.vector.memset(wide_ones[:], 1.0)
        ones = wide_ones[:, 0:P]

        xs = []
        for c in range(8):
            xs.append(keep.tile([P, 1024], BF16, name="xs%d" % c))

        def load_x(c):
            mt, hf = c // 2, c % 2
            nc.sync.dma_start(out=xs[c][:], in_=x_flat[P * mt : P * (mt + 1), 1024 * hf : 1024 * (hf + 1)])

        def load_w(j):
            wd, sd, c0 = groups[j][0], groups[j][1], groups[j][2]
            for q in range(4):
                nc.sync.dma_start(
                    out=planes[j][32 * q : 32 * q + 4, :, :].bitcast(I32),
                    in_=sd[:, 4 * q : 4 * q + 4, c0 : c0 + NB].rearrange("g r n -> r g n").bitcast(I32),
                )
            nc.sync.dma_start(
                out=words[j][:].bitcast(I32),
                in_=wd[:, :, 2 * c0 : 2 * (c0 + NB)].rearrange("g p n -> p g n").bitcast(I32),
            )

        for c in range(4):
            load_x(c)
        load_w(0)
        for c in range(4, 8):
            load_x(c)
        for j in range(1, 6):
            load_w(j)

        rho = THETA ** (-1.0 / HALF)
        nc.vector.tensor_scalar(out=step[:, 1:HALF], in0=step[:, 1:HALF], scalar1=rho, scalar2=None, op0=ALU.mult)
        freq = const.tile([P, HALF], F32, name="freq")
        nc.vector.tensor_tensor_scan(
            out=freq[:], data0=step[:], data1=zero[:], initial=0.5 / math.pi, op0=ALU.mult, op1=ALU.add
        )
        turns = const.tile([P, 2, 2, HALF], F32, name="turns")
        nc.vector.tensor_tensor(
            out=turns[:, :, 1, :], in0=freq[:].unsqueeze(1).to_broadcast([P, 2, HALF]),
            in1=tcol[:].unsqueeze(2).to_broadcast([P, 2, HALF]), op=ALU.mult,
        )
        nc.vector.tensor_scalar(out=turns[:, :, 0, :], in0=turns[:, :, 1, :], scalar1=0.25, scalar2=None, op0=ALU.add)
        turns_f = turns[:].rearrange("p a b d -> p (a b d)")
        whole = const.tile([P, 4 * HALF], I32, name="whole")
        nc.vector.tensor_copy(out=whole[:], in_=turns_f)
        frac = const.tile([P, 4 * HALF], F32, name="frac")
        nc.vector.tensor_tensor(out=frac[:], in0=turns_f, in1=whole[:], op=ALU.subtract)
        nfrac = const.tile([P, 4 * HALF], F32, name="nfrac")
        nc.vector.scalar_tensor_tensor(out=nfrac[:], in0=frac[:], scalar=0.5, in1=frac[:], op0=ALU.is_ge, op1=ALU.subtract)
        trig = const.tile([P, 2, 2, HALF], F32, name="trig")
        nc.scalar.activation(out=trig[:].rearrange("p a b d -> p (a b d)"), in_=nfrac[:], func=ACT.Sin, scale=-2.0 * math.pi)
        nc.scalar.activation(out=warm[:], in_=trig[:, 0, 0, 0:1], func=ACT.Abs_reciprocal_sqrt)
        tab = const.tile([P, 2, 2, 2, DH], F32, name="tab")

        def make_tab(xk):
            nc.vector.tensor_tensor(
                out=tab[:, xk].rearrange("p t k (s d) -> p t k s d", s=2),
                in0=trig[:].unsqueeze(3).to_broadcast([P, 2, 2, 2, HALF]),
                in1=wps[:, xk].rearrange("p k (s d) -> p k s d", s=2).unsqueeze(1).to_broadcast([P, 2, 2, 2, HALF]),
                op=ALU.mult,
            )


        grouped = []
        codes = []
        xscl = []
        for c in range(8):
            grouped.append(keep.tile([P, 2, P, 4], BF16, name="grouped%d" % c, align_bytes=64))
            codes.append(keep.tile([P, 2 * P], U32, name="codes%d" % c, align_bytes=64))
            xscl.append(keep.tile([P, 2 * P], U8, name="xscl%d" % c, align_bytes=64))

        def turn_x(c, eng):
            xw = xs[c][:].bitcast(F32)
            xt = psum.tile([P, 4, P], F32, name="xt", tag="bank")
            for g in range(2):
                for u in range(2):
                    nc.tensor.transpose(xt[:, 2 * g + u, :], xw[:, 256 * g + u : 256 * (g + 1) : 2], ident[:])
            src = xt[:].rearrange("p (g u) r -> p g r u", u=2)
            if eng == 0:
                nc.vector.tensor_copy(out=grouped[c][:].bitcast(F32), in_=src)
            else:
                nc.scalar.copy(out=grouped[c][:].bitcast(F32), in_=src)

        def quant_x(c):
            nc.vector.quantize_mx(
                out=codes[c][:].bitcast(E5X4), scales=xscl[c][:], in_=grouped[c][:].rearrange("p g r t -> p (g r t)")
            )

        idle = psum.tile([P, NB], F32, name="idle", tag="bank")

        def spin(n):
            for i in range(n):
                nc.tensor.matmul(out=idle[:], lhsT=ones, rhs=wide_ones[:], start=True, stop=True)

        with tc.manual_schedule(engines={mybir.EngineType.PE}):
            spin(5)
            turn_x(0, 0)
            turn_x(1, 0)
            quant_x(0)
            quant_x(1)
            spin(1)
            turn_x(2, 1)
            turn_x(3, 1)
            quant_x(2)
            quant_x(3)
            wps = psum.tile([P, 2, 2, DH], F32, name="wps", tag="bank")
            for xk in range(2):
                wrow = wz[:, DH * xk : DH * (xk + 1)]
                nc.tensor.matmul(out=wps[:, xk, 0, :], lhsT=ones, rhs=wrow, start=True, stop=True)
                nc.tensor.matmul(out=wps[:, xk, 1, 0:HALF], lhsT=ones, rhs=wrow[:, 0:HALF], start=True, stop=True)
                nc.tensor.matmul(out=wps[:, xk, 1, HALF:DH], lhsT=neg_ones[:], rhs=wrow[:, HALF:DH], start=True, stop=True)

            spin(4)
        make_tab(0)
        make_tab(1)

        def mm(j, mt):
            acc = psum.tile([P, NB], F32, name="acc", tag="bank")
            for g in range(PASSES):
                c = 2 * mt + g // 2
                cols = slice(P * (g % 2), P * (g % 2 + 1))
                nc.tensor.matmul_mx(
                    out=acc[:],
                    lhsT=codes[c][:, cols].bitcast(E5X4),
                    lhsT_scale=xscl[c][:, cols],
                    rhs=words[j][:, g, :].bitcast(E2X4),
                    rhs_scale=planes[j][:, g, :],
                    start=(g == 0),
                    stop=(g == PASSES - 1),
                )
            return acc

        def squares(acc):
            ss = small.tile([P, 4], F32, name="ss")
            for h in range(4):
                junk = work.tile([P, DH], F32, name="junk")
                nc.scalar.activation(
                    out=junk[:], in_=acc[:, DH * h : DH * (h + 1)], func=ACT.Square, accum_out=ss[:, h : h + 1]
                )
            return ss

        def norm_rope(acc, ss, j, mt):
            tt = mt % 2
            xk = 0 if j < 4 else 1
            rr = small.tile([P, 4], F32, name="rr")
            nc.scalar.activation(out=rr[:], in_=ss[:], func=ACT.Abs_reciprocal_sqrt, scale=1.0 / DH, bias=EPS)
            prod = work.tile([P, 2, 4, DH], F32, name="prod")
            for h in range(4):
                nc.vector.scalar_tensor_tensor(
                    out=prod[:, :, h, :], in0=acc[:, DH * h : DH * (h + 1)].unsqueeze(1).to_broadcast([P, 2, DH]),
                    scalar=rr[:, h : h + 1], in1=tab[:, xk, tt], op0=ALU.mult, op1=ALU.mult,
                )
            return prod

        def add_store(adder, prod, j, mt):
            p5 = prod[:].rearrange("p k h (s d) -> p k h s d", s=2)
            o = outp.tile([P, NB], F32, name="o")
            adder.tensor_tensor(
                out=o[:].rearrange("p (h s d) -> p h s d", h=4, s=2), in0=p5[:, 0], in1=p5[:, 1, :, ::-1, :], op=ALU.add
            )
            dst, d0 = groups[j][3], groups[j][4]
            nc.sync.dma_start(out=dst[P * mt : P * (mt + 1), d0 : d0 + NB], in_=o[:])

        ctx.enter_context(
            tc.manual_schedule(engines={mybir.EngineType.PE, mybir.EngineType.Activation, mybir.EngineType.DVE})
        )
        late = []
        for j in range(6):
            for mt in range(4):
                acc = mm(j, mt)
                if j < 5:
                    prod = norm_rope(acc, squares(acc), j, mt)
                for args in late:
                    add_store(nc.vector, *args)
                late.clear()
                if j == 5:
                    o = outp.tile([P, NB], F32, name="o")
                    nc.scalar.copy(out=o[:], in_=acc[:])
                    nc.sync.dma_start(out=v_flat[P * mt : P * (mt + 1), :], in_=o[:])
                elif (4 * j + mt) % 10 == 9:
                    late.append((prod, j, mt))
                else:
                    add_store(nc.gpsimd, prod, j, mt)
                if j == 0 and mt < 2:
                    turn_x(2 * mt + 4, 1)
                    turn_x(2 * mt + 5, 1)
                    quant_x(2 * mt + 4)
                    quant_x(2 * mt + 5)
                if j == 0 and mt in (1, 2):
                    spin(6 - 2 * mt)
